import numpy as np
import ml_dtypes


def mxq(x, axis, fmt="e4m3"):
    dtype, down = {"e4m3": (ml_dtypes.float8_e4m3fn, 7), "e5m2": (ml_dtypes.float8_e5m2, 14)}[fmt]
    v = np.moveaxis(np.asarray(x, np.float32).astype(ml_dtypes.bfloat16).astype(np.float64), axis, -1)
    blocks = v.reshape(v.shape[:-1] + (-1, 32))
    amax = np.abs(blocks).max(-1, keepdims=True)
    byte = np.maximum(np.where(amax > 0, np.frexp(amax)[1] - 1 + 127, 0) - down, 1)
    scale = np.exp2(byte - 127.0)
    codes = (blocks / scale).astype(np.float32).astype(dtype).astype(np.float64)
    return np.moveaxis((codes * scale).reshape(v.shape), -1, axis)


WIDE = False


def mx_kscale(k):
    if not WIDE:
        return np.ones(k)
    levels = np.array([10, -10, 5, -5, 0])
    a = np.random.permutation(np.resize(levels, k // 512 * 4)).reshape(k // 512, 4)
    idx = np.arange(k)
    return np.exp2(a[idx // 512, idx % 128 // 32])


BF16 = ml_dtypes.bfloat16


def bf(x):
    return np.asarray(x, np.float32).astype(BF16)


def f64(x):
    return np.asarray(x).astype(np.float64)


B, D_IN, D_H = 4096, 512, 512


def sigmoid(v):
    return 1.0 / (1.0 + np.exp(-v))


def setup_inputs():
    s, t = mx_kscale(D_IN), mx_kscale(D_H)

    def w_in():
        return bf(np.random.standard_normal((D_H, D_IN)) * 0.6 / np.sqrt(D_IN) / s[None, :])

    def w_rec():
        return bf(np.random.standard_normal((D_H, D_H)) * 0.6 / np.sqrt(D_H) / t[None, :])

    def bias():
        return bf(np.random.standard_normal(D_H) * 0.3)

    return {"incoming": bf(np.random.standard_normal((B, D_IN)) * s), "h": bf(np.random.standard_normal((B, D_H)) * t),
            "W_i": w_in(), "b_W_i": bias(), "W_c": w_in(), "b_W_c": bias(),
            "U_i": w_rec(), "b_U_i": bias(), "U_c": w_rec(), "b_U_c": bias()}


def reference(incoming, h, W_i, b_W_i, W_c, b_W_c, U_i, b_U_i, U_c, b_U_c):
    xq = mxq(f64(incoming), 1, "e4m3")
    hq = mxq(f64(h), 1, "e4m3")
    I = sigmoid((xq @ mxq(f64(W_i), 1, "e4m3").T) + f64(b_W_i) + (hq @ mxq(f64(U_i), 1, "e4m3").T) + f64(b_U_i))
    C_head = (xq @ mxq(f64(W_c), 1, "e4m3").T) + f64(b_W_c) + (hq @ mxq(f64(U_c), 1, "e4m3").T) + f64(b_U_c)
    return I * C_head

@@ -1,0 +1,194 @@
+from contextlib import ExitStack
+
+import concourse.masks as masks
+import concourse.mybir as mybir
+
+F32 = mybir.dt.float32
+BF16 = mybir.dt.bfloat16
+U32 = mybir.dt.uint32
+U8 = mybir.dt.uint8
+FP8X4 = mybir.dt.float8_e4m3fn_x4
+ADD = mybir.AluOpType.add
+MULT = mybir.AluOpType.mult
+SIGMOID = mybir.ActivationFunctionType.Sigmoid
+
+P = 128
+BATCH = 4096
+K = 512
+D_H = 512
+WORDS = K // 2
+PAIR = 2 * P
+
+TILES_PER_LOAD = 4
+N_LOADS = BATCH // (P * TILES_PER_LOAD)
+ROUND = 2
+N_ROUNDS = BATCH // (P * ROUND)
+BANKS = ROUND
+
+FLOPS = 2 * BATCH * K * D_H * 4
+
+
+def tile_lstmcell_pa_t_kernel(
+    tc, incoming, h, W_i, b_W_i, W_c, b_W_c, U_i, b_U_i, U_c, b_U_c, out
+):
+    nc = tc.nc
+    with ExitStack() as ctx:
+        consts = ctx.enter_context(tc.tile_pool(name="consts", bufs=1))
+        acts = ctx.enter_context(tc.tile_pool(name="acts", bufs=N_LOADS))
+        w_stage = ctx.enter_context(tc.tile_pool(name="w_stage", bufs=4))
+        quant = ctx.enter_context(tc.tile_pool(name="quant", bufs=3))
+        epilogue = ctx.enter_context(tc.tile_pool(name="epilogue", bufs=4))
+        words_psum = ctx.enter_context(tc.psum_pool(name="words_psum", bufs=4))
+        sums_psum = ctx.enter_context(tc.psum_pool(name="sums_psum", bufs=2))
+        ctx.enter_context(tc.manual_schedule())
+
+        ident = consts.tile([P, P], F32)
+        masks.make_identity(nc, ident[:])
+        ones = consts.tile([P, P], BF16)
+        nc.vector.memset(ones[:], 1.0)
+        bias_rows = consts.tile([P, 2 * D_H], BF16)
+        nc.vector.memset(bias_rows[:], 0.0)
+        for row, (b_i, b_c) in enumerate(((b_W_i, b_W_c), (b_U_i, b_U_c))):
+            nc.scalar.dma_start(out=bias_rows[row : row + 1, 0:D_H], in_=b_i.unsqueeze(0))
+            nc.scalar.dma_start(out=bias_rows[row : row + 1, D_H : 2 * D_H], in_=b_c.unsqueeze(0))
+        table_warmer = consts.tile([P, 1], F32)
+        nc.vector.memset(table_warmer[:], 0.0)
+        nc.scalar.activation(out=table_warmer[:], in_=table_warmer[:], func=SIGMOID)
+
+        x_view = incoming.rearrange("(c p j) k -> c p (j k)", p=P, j=TILES_PER_LOAD)
+        h_view = h.rearrange("(c p j) k -> c p (j k)", p=P, j=TILES_PER_LOAD)
+        out_view = out.rearrange("(c p j) f -> c p j f", p=P, j=TILES_PER_LOAD)
+        act_words = []
+
+        def load_activations(c):
+            x_rows = acts.tile([P, TILES_PER_LOAD * K], BF16)
+            nc.sync.dma_start(out=x_rows[:], in_=x_view[c])
+            h_rows = acts.tile([P, TILES_PER_LOAD * K], BF16)
+            nc.sync.dma_start(out=h_rows[:], in_=h_view[c])
+            act_words.append((x_rows[:].bitcast(F32), h_rows[:].bitcast(F32)))
+
+        load_activations(0)
+        weight_words = []
+        for w in (W_i, U_i, W_c, U_c):
+            w_rows = w_stage.tile([P, (D_H // P) * K], BF16)
+            nc.sync.dma_start(
+                out=w_rows[:].rearrange("p (r k) -> p r k", k=K),
+                in_=w.rearrange("(r p) k -> p r k", p=P),
+            )
+            weight_words.append(w_rows[:].bitcast(F32))
+        for c in range(1, N_LOADS):
+            load_activations(c)
+
+        def transpose_pair(words):
+            bank = words_psum.tile([P, 2, PAIR], F32)
+            for s in range(2):
+                for u in range(2):
+                    nc.tensor.transpose(
+                        out=bank[:, u, s * P : (s + 1) * P],
+                        in_=words[:, (2 * s + u) * P : (2 * s + u + 1) * P],
+                        identity=ident[:],
+                    )
+            return bank
+
+        def regroup(copy, bank, grouped, b):
+            copy(
+                out=grouped[:]
+                .bitcast(F32)[:, b * 2 * PAIR : (b + 1) * 2 * PAIR]
+                .rearrange("p (r u) -> p r u", u=2),
+                in_=bank[:].rearrange("p u r -> p r u"),
+            )
+
+        word_banks = {}
+        grouped_tiles = {}
+        packed = {}
+
+        def transpose_round(u):
+            first_pair = u * (ROUND // 2)
+            word_banks[u] = []
+            for operand in range(2):
+                for pair in range(first_pair, first_pair + ROUND // 2):
+                    words = act_words[pair // 2][operand]
+                    half = (pair % 2) * 2 * WORDS
+                    word_banks[u].append(transpose_pair(words[:, half : half + 2 * WORDS]))
+            grouped = quant.tile([P, 2 * ROUND * P * 4], BF16, align_bytes=64)
+            grouped_tiles[u] = grouped
+
+        def quantise_round(u):
+            codes = quant.tile([P, 2 * ROUND * P], U32, align_bytes=64)
+            scales = quant.tile([P, 2 * ROUND * P], U8, align_bytes=64)
+            nc.vector.quantize_mx(
+                out=codes[:].bitcast(FP8X4), scales=scales[:], in_=grouped_tiles[u][:]
+            )
+            packed[u] = (codes, scales)
+
+        def gate_sums(u, i, gate):
+            codes, scales = packed[u]
+            sums = sums_psum.tile([P, D_H], F32, tag="sums_%d" % gate)
+            for operand in range(2):
+                rows = slice((operand * ROUND + i) * P, (operand * ROUND + i + 1) * P)
+                nc.tensor.matmul_mx(
+                    out=sums[:],
+                    lhsT=codes[:, rows].bitcast(FP8X4),
+                    lhsT_scale=scales[:, rows],
+                    rhs=w_codes[:, 2 * gate + operand, :].bitcast(FP8X4),
+                    rhs_scale=w_scales[:, 2 * gate + operand, :],
+                    start=(operand == 0),
+                    stop=(operand == 1),
+                )
+            return sums
+
+        head_copies = (nc.scalar.copy, nc.vector.tensor_copy)
+        for u in range(2):
+            transpose_round(u)
+            for b in range(BANKS):
+                regroup(head_copies[b % 2], word_banks[u][b], grouped_tiles[u], b)
+
+        bias = consts.tile([P, 2, D_H], F32)
+        for gate in range(2):
+            spread = sums_psum.tile([P, D_H], F32, tag="sums_%d" % gate)
+            nc.tensor.matmul(
+                out=spread[:],
+                lhsT=ones[:],
+                rhs=bias_rows[:, gate * D_H : (gate + 1) * D_H],
+                start=True,
+                stop=True,
+            )
+            nc.vector.tensor_copy(out=bias[:, gate, :], in_=spread[:])
+        quantise_round(0)
+
+        w_codes = consts.tile([P, 4, D_H], U32, align_bytes=64)
+        w_scales = consts.tile([P, 4, D_H], U8, align_bytes=64)
+        for m in range(4):
+            w_grouped = w_stage.tile([P, D_H * 4], BF16, align_bytes=64)
+            for b in range(2):
+                bank = transpose_pair(weight_words[m][:, b * 2 * WORDS : (b + 1) * 2 * WORDS])
+                regroup(head_copies[b % 2], bank, w_grouped, b)
+            nc.vector.quantize_mx(
+                out=w_codes[:, m, :].bitcast(FP8X4), scales=w_scales[:, m, :], in_=w_grouped[:]
+            )
+
+        for u in range(N_ROUNDS):
+            if u + 2 < N_ROUNDS:
+                transpose_round(u + 2)
+            if u + 1 < N_ROUNDS:
+                quantise_round(u + 1)
+            result = epilogue.tile([P, ROUND, D_H], F32)
+            for i in range(ROUND):
+                sums_i = gate_sums(u, i, 0)
+                sums_c = gate_sums(u, i, 1)
+                gate_i = epilogue.tile([P, D_H], F32)
+                nc.vector.tensor_tensor(out=gate_i[:], in0=sums_i[:], in1=bias[:, 0, :], op=ADD)
+                if u + 2 < N_ROUNDS:
+                    regroup(nc.scalar.copy, word_banks[u + 2][i], grouped_tiles[u + 2], i)
+                nc.scalar.activation(out=gate_i[:], in_=gate_i[:], func=SIGMOID)
+                nc.vector.tensor_tensor(
+                    out=result[:, i, :], in0=sums_c[:], in1=bias[:, 1, :], op=ADD
+                )
+                nc.gpsimd.tensor_tensor(
+                    out=result[:, i, :], in0=result[:, i, :], in1=gate_i[:], op=MULT
+                )
+            first_tile = u * ROUND
+            j = first_tile % TILES_PER_LOAD
+            nc.sync.dma_start(
+                out=out_view[first_tile // TILES_PER_LOAD, :, j : j + ROUND, :], in_=result[:]
+            )

@@ -167,12 +167,29 @@ def tile_lstmcell_pa_t_kernel(
                 out=w_codes[:, m, :].bitcast(FP8X4), scales=w_scales[:, m, :], in_=w_grouped[:]
             )
 
+        unfinished = {}
+
+        def finish_round(u):
+            result, odd_gates = unfinished[u]
+            for i, gate_i in odd_gates:
+                nc.vector.tensor_tensor(
+                    out=result[:, i, :], in0=result[:, i, :], in1=gate_i[:], op=MULT
+                )
+            first_tile = u * ROUND
+            j = first_tile % TILES_PER_LOAD
+            nc.sync.dma_start(
+                out=out_view[first_tile // TILES_PER_LOAD, :, j : j + ROUND, :], in_=result[:]
+            )
+
         for u in range(N_ROUNDS):
             if u + 2 < N_ROUNDS:
                 transpose_round(u + 2)
             if u + 1 < N_ROUNDS:
                 quantise_round(u + 1)
+            if u > 0:
+                finish_round(u - 1)
             result = epilogue.tile([P, ROUND, D_H], F32)
+            unfinished[u] = (result, [])
             for i in range(ROUND):
                 sums_i = gate_sums(u, i, 0)
                 sums_c = gate_sums(u, i, 1)
@@ -184,11 +201,10 @@ def tile_lstmcell_pa_t_kernel(
                 nc.vector.tensor_tensor(
                     out=result[:, i, :], in0=sums_c[:], in1=bias[:, 1, :], op=ADD
                 )
-                nc.gpsimd.tensor_tensor(
-                    out=result[:, i, :], in0=result[:, i, :], in1=gate_i[:], op=MULT
-                )
-            first_tile = u * ROUND
-            j = first_tile % TILES_PER_LOAD
-            nc.sync.dma_start(
-                out=out_view[first_tile // TILES_PER_LOAD, :, j : j + ROUND, :], in_=result[:]
-            )
+                if i % 2 == 0:
+                    nc.gpsimd.tensor_tensor(
+                        out=result[:, i, :], in0=result[:, i, :], in1=gate_i[:], op=MULT
+                    )
+                else:
+                    unfinished[u][1].append((i, gate_i))
+        finish_round(N_ROUNDS - 1)

@@ -16,14 +16,10 @@ P = 128
 BATCH = 4096
 K = 512
 D_H = 512
-WORDS = K // 2
-PAIR = 2 * P
-
-TILES_PER_LOAD = 4
-N_LOADS = BATCH // (P * TILES_PER_LOAD)
-ROUND = 2
-N_ROUNDS = BATCH // (P * ROUND)
-BANKS = ROUND
+PAIR = 2
+PAIR_ROWS = PAIR * P
+PAIR_WORDS = PAIR * K // 2
+N_ROUNDS = BATCH // PAIR_ROWS
 
 FLOPS = 2 * BATCH * K * D_H * 4
 
@@ -34,10 +30,11 @@ def tile_lstmcell_pa_t_kernel(
     nc = tc.nc
     with ExitStack() as ctx:
         consts = ctx.enter_context(tc.tile_pool(name="consts", bufs=1))
-        acts = ctx.enter_context(tc.tile_pool(name="acts", bufs=N_LOADS))
+        acts = ctx.enter_context(tc.tile_pool(name="acts", bufs=N_ROUNDS))
         w_stage = ctx.enter_context(tc.tile_pool(name="w_stage", bufs=4))
         quant = ctx.enter_context(tc.tile_pool(name="quant", bufs=3))
-        epilogue = ctx.enter_context(tc.tile_pool(name="epilogue", bufs=4))
+        gates = ctx.enter_context(tc.tile_pool(name="gates", bufs=4))
+        results = ctx.enter_context(tc.tile_pool(name="results", bufs=10))
         words_psum = ctx.enter_context(tc.psum_pool(name="words_psum", bufs=4))
         sums_psum = ctx.enter_context(tc.psum_pool(name="sums_psum", bufs=2))
         ctx.enter_context(tc.manual_schedule())
@@ -55,19 +52,19 @@ def tile_lstmcell_pa_t_kernel(
         nc.vector.memset(table_warmer[:], 0.0)
         nc.scalar.activation(out=table_warmer[:], in_=table_warmer[:], func=SIGMOID)
 
-        x_view = incoming.rearrange("(c p j) k -> c p (j k)", p=P, j=TILES_PER_LOAD)
-        h_view = h.rearrange("(c p j) k -> c p (j k)", p=P, j=TILES_PER_LOAD)
-        out_view = out.rearrange("(c p j) f -> c p j f", p=P, j=TILES_PER_LOAD)
+        x_view = incoming.rearrange("(n p i) k -> n p (i k)", p=P, i=PAIR)
+        h_view = h.rearrange("(n p i) k -> n p (i k)", p=P, i=PAIR)
+        out_view = out.rearrange("(n p i) f -> n p i f", p=P, i=PAIR)
         act_words = []
 
-        def load_activations(c):
-            x_rows = acts.tile([P, TILES_PER_LOAD * K], BF16)
-            nc.sync.dma_start(out=x_rows[:], in_=x_view[c])
-            h_rows = acts.tile([P, TILES_PER_LOAD * K], BF16)
-            nc.sync.dma_start(out=h_rows[:], in_=h_view[c])
+        def load_round(n):
+            x_rows = acts.tile([P, PAIR * K], BF16)
+            nc.sync.dma_start(out=x_rows[:], in_=x_view[n])
+            h_rows = acts.tile([P, PAIR * K], BF16)
+            nc.sync.dma_start(out=h_rows[:], in_=h_view[n])
             act_words.append((x_rows[:].bitcast(F32), h_rows[:].bitcast(F32)))
 
-        load_activations(0)
+        load_round(0)
         weight_words = []
         for w in (W_i, U_i, W_c, U_c):
             w_rows = w_stage.tile([P, (D_H // P) * K], BF16)
@@ -76,12 +73,12 @@ def tile_lstmcell_pa_t_kernel(
                 in_=w.rearrange("(r p) k -> p r k", p=P),
             )
             weight_words.append(w_rows[:].bitcast(F32))
-        for c in range(1, N_LOADS):
-            load_activations(c)
+        for n in range(1, N_ROUNDS):
+            load_round(n)
 
         def transpose_pair(words):
-            bank = words_psum.tile([P, 2, PAIR], F32)
-            for s in range(2):
+            bank = words_psum.tile([P, 2, PAIR_ROWS], F32)
+            for s in range(PAIR):
                 for u in range(2):
                     nc.tensor.transpose(
                         out=bank[:, u, s * P : (s + 1) * P],
@@ -93,7 +90,7 @@ def tile_lstmcell_pa_t_kernel(
         def regroup(copy, bank, grouped, b):
             copy(
                 out=grouped[:]
-                .bitcast(F32)[:, b * 2 * PAIR : (b + 1) * 2 * PAIR]
+                .bitcast(F32)[:, b * PAIR_WORDS : (b + 1) * PAIR_WORDS]
                 .rearrange("p (r u) -> p r u", u=2),
                 in_=bank[:].rearrange("p u r -> p r u"),
             )
@@ -102,30 +99,27 @@ def tile_lstmcell_pa_t_kernel(
         grouped_tiles = {}
         packed = {}
 
-        def transpose_round(u):
-            first_pair = u * (ROUND // 2)
-            word_banks[u] = []
-            for operand in range(2):
-                for pair in range(first_pair, first_pair + ROUND // 2):
-                    words = act_words[pair // 2][operand]
-                    half = (pair % 2) * 2 * WORDS
-                    word_banks[u].append(transpose_pair(words[:, half : half + 2 * WORDS]))
-            grouped = quant.tile([P, 2 * ROUND * P * 4], BF16, align_bytes=64)
-            grouped_tiles[u] = grouped
+        def transpose_round(n):
+            word_banks[n] = [transpose_pair(words) for words in act_words[n]]
+            grouped = quant.tile([P, 2 * PAIR_ROWS * 4], BF16, align_bytes=64)
+            grouped_tiles[n] = grouped
 
-        def quantise_round(u):
-            codes = quant.tile([P, 2 * ROUND * P], U32, align_bytes=64)
-            scales = quant.tile([P, 2 * ROUND * P], U8, align_bytes=64)
+        def regroup_operand(n, operand):
+            regroup(nc.scalar.copy, word_banks[n][operand], grouped_tiles[n], operand)
+
+        def quantise_round(n):
+            codes = quant.tile([P, 2 * PAIR_ROWS], U32, align_bytes=64)
+            scales = quant.tile([P, 2 * PAIR_ROWS], U8, align_bytes=64)
             nc.vector.quantize_mx(
-                out=codes[:].bitcast(FP8X4), scales=scales[:], in_=grouped_tiles[u][:]
+                out=codes[:].bitcast(FP8X4), scales=scales[:], in_=grouped_tiles[n][:]
             )
-            packed[u] = (codes, scales)
+            packed[n] = (codes, scales)
 
-        def gate_sums(u, i, gate):
-            codes, scales = packed[u]
+        def gate_sums(n, i, gate):
+            codes, scales = packed[n]
             sums = sums_psum.tile([P, D_H], F32, tag="sums_%d" % gate)
             for operand in range(2):
-                rows = slice((operand * ROUND + i) * P, (operand * ROUND + i + 1) * P)
+                rows = slice((operand * PAIR + i) * P, (operand * PAIR + i + 1) * P)
                 nc.tensor.matmul_mx(
                     out=sums[:],
                     lhsT=codes[:, rows].bitcast(FP8X4),
@@ -137,11 +131,9 @@ def tile_lstmcell_pa_t_kernel(
                 )
             return sums
 
-        head_copies = (nc.scalar.copy, nc.vector.tensor_copy)
-        for u in range(2):
-            transpose_round(u)
-            for b in range(BANKS):
-                regroup(head_copies[b % 2], word_banks[u][b], grouped_tiles[u], b)
+        transpose_round(0)
+        for operand in range(2):
+            regroup_operand(0, operand)
 
         bias = consts.tile([P, 2, D_H], F32)
         for gate in range(2):
@@ -160,51 +152,31 @@ def tile_lstmcell_pa_t_kernel(
         w_scales = consts.tile([P, 4, D_H], U8, align_bytes=64)
         for m in range(4):
             w_grouped = w_stage.tile([P, D_H * 4], BF16, align_bytes=64)
-            for b in range(2):
-                bank = transpose_pair(weight_words[m][:, b * 2 * WORDS : (b + 1) * 2 * WORDS])
-                regroup(head_copies[b % 2], bank, w_grouped, b)
+            for b, copy in enumerate((nc.scalar.copy, nc.vector.tensor_copy)):
+                bank = transpose_pair(weight_words[m][:, b * PAIR_WORDS : (b + 1) * PAIR_WORDS])
+                regroup(copy, bank, w_grouped, b)
             nc.vector.quantize_mx(
                 out=w_codes[:, m, :].bitcast(FP8X4), scales=w_scales[:, m, :], in_=w_grouped[:]
             )
 
-        unfinished = {}
+        transpose_round(1)
+        for operand in range(2):
+            regroup_operand(1, operand)
 
-        def finish_round(u):
-            result, odd_gates = unfinished[u]
-            for i, gate_i in odd_gates:
-                nc.vector.tensor_tensor(
-                    out=result[:, i, :], in0=result[:, i, :], in1=gate_i[:], op=MULT
-                )
-            first_tile = u * ROUND
-            j = first_tile % TILES_PER_LOAD
-            nc.sync.dma_start(
-                out=out_view[first_tile // TILES_PER_LOAD, :, j : j + ROUND, :], in_=result[:]
-            )
-
-        for u in range(N_ROUNDS):
-            if u + 2 < N_ROUNDS:
-                transpose_round(u + 2)
-            if u + 1 < N_ROUNDS:
-                quantise_round(u + 1)
-            if u > 0:
-                finish_round(u - 1)
-            result = epilogue.tile([P, ROUND, D_H], F32)
-            unfinished[u] = (result, [])
-            for i in range(ROUND):
-                sums_i = gate_sums(u, i, 0)
-                sums_c = gate_sums(u, i, 1)
-                gate_i = epilogue.tile([P, D_H], F32)
+        for n in range(N_ROUNDS):
+            if n + 1 < N_ROUNDS:
+                quantise_round(n + 1)
+            sums = [(gate_sums(n, 0, 0), gate_sums(n, 0, 1))]
+            if n + 2 < N_ROUNDS:
+                transpose_round(n + 2)
+            sums.append((gate_sums(n, 1, 0), gate_sums(n, 1, 1)))
+            for i, (sums_i, sums_c) in enumerate(sums):
+                gate_i = gates.tile([P, D_H], F32)
                 nc.vector.tensor_tensor(out=gate_i[:], in0=sums_i[:], in1=bias[:, 0, :], op=ADD)
-                if u + 2 < N_ROUNDS:
-                    regroup(nc.scalar.copy, word_banks[u + 2][i], grouped_tiles[u + 2], i)
+                if n + 2 < N_ROUNDS:
+                    regroup_operand(n + 2, i)
                 nc.scalar.activation(out=gate_i[:], in_=gate_i[:], func=SIGMOID)
-                nc.vector.tensor_tensor(
-                    out=result[:, i, :], in0=sums_c[:], in1=bias[:, 1, :], op=ADD
-                )
-                if i % 2 == 0:
-                    nc.gpsimd.tensor_tensor(
-                        out=result[:, i, :], in0=result[:, i, :], in1=gate_i[:], op=MULT
-                    )
-                else:
-                    unfinished[u][1].append((i, gate_i))
-        finish_round(N_ROUNDS - 1)
+                result = results.tile([P, D_H], F32)
+                nc.vector.tensor_tensor(out=result[:], in0=sums_c[:], in1=bias[:, 1, :], op=ADD)
+                nc.gpsimd.tensor_tensor(out=result[:], in0=result[:], in1=gate_i[:], op=MULT)
+                nc.sync.dma_start(out=out_view[n, :, i, :], in_=result[:])

from contextlib import ExitStack

import concourse.masks as masks
import concourse.mybir as mybir

F32 = mybir.dt.float32
BF16 = mybir.dt.bfloat16
U32 = mybir.dt.uint32
U8 = mybir.dt.uint8
FP8X4 = mybir.dt.float8_e4m3fn_x4
ADD = mybir.AluOpType.add
MULT = mybir.AluOpType.mult
SIGMOID = mybir.ActivationFunctionType.Sigmoid

P = 128
BATCH = 4096
K = 512
D_H = 512
PAIR = 2
PAIR_ROWS = PAIR * P
PAIR_WORDS = PAIR * K // 2
N_ROUNDS = BATCH // PAIR_ROWS

FLOPS = 2 * BATCH * K * D_H * 4


def tile_lstmcell_pa_t_kernel(
    tc, incoming, h, W_i, b_W_i, W_c, b_W_c, U_i, b_U_i, U_c, b_U_c, out
):
    nc = tc.nc
    with ExitStack() as ctx:
        consts = ctx.enter_context(tc.tile_pool(name="consts", bufs=1))
        acts = ctx.enter_context(tc.tile_pool(name="acts", bufs=N_ROUNDS))
        w_stage = ctx.enter_context(tc.tile_pool(name="w_stage", bufs=4))
        quant = ctx.enter_context(tc.tile_pool(name="quant", bufs=3))
        gates = ctx.enter_context(tc.tile_pool(name="gates", bufs=4))
        results = ctx.enter_context(tc.tile_pool(name="results", bufs=10))
        words_psum = ctx.enter_context(tc.psum_pool(name="words_psum", bufs=4))
        sums_psum = ctx.enter_context(tc.psum_pool(name="sums_psum", bufs=2))
        ctx.enter_context(tc.manual_schedule())

        ident = consts.tile([P, P], F32)
        masks.make_identity(nc, ident[:])
        ones = consts.tile([P, P], BF16)
        nc.vector.memset(ones[:], 1.0)
        bias_rows = consts.tile([P, 2 * D_H], BF16)
        nc.vector.memset(bias_rows[:], 0.0)
        for row, (b_i, b_c) in enumerate(((b_W_i, b_W_c), (b_U_i, b_U_c))):
            nc.scalar.dma_start(out=bias_rows[row : row + 1, 0:D_H], in_=b_i.unsqueeze(0))
            nc.scalar.dma_start(out=bias_rows[row : row + 1, D_H : 2 * D_H], in_=b_c.unsqueeze(0))
        table_warmer = consts.tile([P, 1], F32)
        nc.vector.memset(table_warmer[:], 0.0)
        nc.scalar.activation(out=table_warmer[:], in_=table_warmer[:], func=SIGMOID)

        x_view = incoming.rearrange("(n p i) k -> n p (i k)", p=P, i=PAIR)
        h_view = h.rearrange("(n p i) k -> n p (i k)", p=P, i=PAIR)
        out_view = out.rearrange("(n p i) f -> n p i f", p=P, i=PAIR)
        act_words = []

        def load_round(n):
            x_rows = acts.tile([P, PAIR * K], BF16)
            nc.sync.dma_start(out=x_rows[:], in_=x_view[n])
            h_rows = acts.tile([P, PAIR * K], BF16)
            nc.sync.dma_start(out=h_rows[:], in_=h_view[n])
            act_words.append((x_rows[:].bitcast(F32), h_rows[:].bitcast(F32)))

        load_round(0)
        weight_words = []
        for w in (W_i, U_i, W_c, U_c):
            w_rows = w_stage.tile([P, (D_H // P) * K], BF16)
            nc.sync.dma_start(
                out=w_rows[:].rearrange("p (r k) -> p r k", k=K),
                in_=w.rearrange("(r p) k -> p r k", p=P),
            )
            weight_words.append(w_rows[:].bitcast(F32))
        for n in range(1, N_ROUNDS):
            load_round(n)

        def transpose_pair(words):
            bank = words_psum.tile([P, 2, PAIR_ROWS], F32)
            for s in range(PAIR):
                for u in range(2):
                    nc.tensor.transpose(
                        out=bank[:, u, s * P : (s + 1) * P],
                        in_=words[:, (2 * s + u) * P : (2 * s + u + 1) * P],
                        identity=ident[:],
                    )
            return bank

        def regroup(copy, bank, grouped, b):
            copy(
                out=grouped[:]
                .bitcast(F32)[:, b * PAIR_WORDS : (b + 1) * PAIR_WORDS]
                .rearrange("p (r u) -> p r u", u=2),
                in_=bank[:].rearrange("p u r -> p r u"),
            )

        word_banks = {}
        grouped_tiles = {}
        packed = {}

        def transpose_round(n):
            word_banks[n] = [transpose_pair(words) for words in act_words[n]]
            grouped = quant.tile([P, 2 * PAIR_ROWS * 4], BF16, align_bytes=64)
            grouped_tiles[n] = grouped

        def regroup_operand(n, operand):
            regroup(nc.scalar.copy, word_banks[n][operand], grouped_tiles[n], operand)

        def quantise_round(n):
            codes = quant.tile([P, 2 * PAIR_ROWS], U32, align_bytes=64)
            scales = quant.tile([P, 2 * PAIR_ROWS], U8, align_bytes=64)
            nc.vector.quantize_mx(
                out=codes[:].bitcast(FP8X4), scales=scales[:], in_=grouped_tiles[n][:]
            )
            packed[n] = (codes, scales)

        def gate_sums(n, i, gate):
            codes, scales = packed[n]
            sums = sums_psum.tile([P, D_H], F32, tag="sums_%d" % gate)
            for operand in range(2):
                rows = slice((operand * PAIR + i) * P, (operand * PAIR + i + 1) * P)
                nc.tensor.matmul_mx(
                    out=sums[:],
                    lhsT=codes[:, rows].bitcast(FP8X4),
                    lhsT_scale=scales[:, rows],
                    rhs=w_codes[:, 2 * gate + operand, :].bitcast(FP8X4),
                    rhs_scale=w_scales[:, 2 * gate + operand, :],
                    start=(operand == 0),
                    stop=(operand == 1),
                )
            return sums

        transpose_round(0)
        for operand in range(2):
            regroup_operand(0, operand)

        bias = consts.tile([P, 2, D_H], F32)
        for gate in range(2):
            spread = sums_psum.tile([P, D_H], F32, tag="sums_%d" % gate)
            nc.tensor.matmul(
                out=spread[:],
                lhsT=ones[:],
                rhs=bias_rows[:, gate * D_H : (gate + 1) * D_H],
                start=True,
                stop=True,
            )
            nc.vector.tensor_copy(out=bias[:, gate, :], in_=spread[:])
        quantise_round(0)

        w_codes = consts.tile([P, 4, D_H], U32, align_bytes=64)
        w_scales = consts.tile([P, 4, D_H], U8, align_bytes=64)
        for m in range(4):
            w_grouped = w_stage.tile([P, D_H * 4], BF16, align_bytes=64)
            for b, copy in enumerate((nc.scalar.copy, nc.vector.tensor_copy)):
                bank = transpose_pair(weight_words[m][:, b * PAIR_WORDS : (b + 1) * PAIR_WORDS])
                regroup(copy, bank, w_grouped, b)
            nc.vector.quantize_mx(
                out=w_codes[:, m, :].bitcast(FP8X4), scales=w_scales[:, m, :], in_=w_grouped[:]
            )

        transpose_round(1)
        for operand in range(2):
            regroup_operand(1, operand)

        for n in range(N_ROUNDS):
            if n + 1 < N_ROUNDS:
                quantise_round(n + 1)
            sums = [(gate_sums(n, 0, 0), gate_sums(n, 0, 1))]
            if n + 2 < N_ROUNDS:
                transpose_round(n + 2)
            sums.append((gate_sums(n, 1, 0), gate_sums(n, 1, 1)))
            for i, (sums_i, sums_c) in enumerate(sums):
                gate_i = gates.tile([P, D_H], F32)
                nc.vector.tensor_tensor(out=gate_i[:], in0=sums_i[:], in1=bias[:, 0, :], op=ADD)
                if n + 2 < N_ROUNDS:
                    regroup_operand(n + 2, i)
                nc.scalar.activation(out=gate_i[:], in_=gate_i[:], func=SIGMOID)
                result = results.tile([P, D_H], F32)
                nc.vector.tensor_tensor(out=result[:], in0=sums_c[:], in1=bias[:, 1, :], op=ADD)
                nc.gpsimd.tensor_tensor(out=result[:], in0=result[:], in1=gate_i[:], op=MULT)
                nc.sync.dma_start(out=out_view[n, :, i, :], in_=result[:])
